import numpy as np
import ml_dtypes


def mxq(x, axis, fmt="e4m3"):
    dtype, down = {"e4m3": (ml_dtypes.float8_e4m3fn, 7), "e5m2": (ml_dtypes.float8_e5m2, 14)}[fmt]
    v = np.moveaxis(np.asarray(x, np.float32).astype(ml_dtypes.bfloat16).astype(np.float64), axis, -1)
    blocks = v.reshape(v.shape[:-1] + (-1, 32))
    amax = np.abs(blocks).max(-1, keepdims=True)
    byte = np.maximum(np.where(amax > 0, np.frexp(amax)[1] - 1 + 127, 0) - down, 1)
    scale = np.exp2(byte - 127.0)
    codes = (blocks / scale).astype(np.float32).astype(dtype).astype(np.float64)
    return np.moveaxis((codes * scale).reshape(v.shape), -1, axis)


WIDE = False


def mx_kscale(k):
    if not WIDE:
        return np.ones(k)
    levels = np.array([10, -10, 5, -5, 0])
    a = np.random.permutation(np.resize(levels, k // 512 * 4)).reshape(k // 512, 4)
    idx = np.arange(k)
    return np.exp2(a[idx // 512, idx % 128 // 32])


BF16 = ml_dtypes.bfloat16


def bf(x):
    return np.asarray(x, np.float32).astype(BF16)


def f64(x):
    return np.asarray(x).astype(np.float64)


B, A, E, P, R = 1024, 8, 1024, 512, 256


def setup_inputs():
    s_src, s_edge = mx_kscale(E), mx_kscale(E)
    t = mx_kscale(P)
    s_cat = np.concatenate([s_src, s_edge])
    return {
        "image_features": bf(np.random.standard_normal((B, E)) * s_src),
        "edge_attributes": bf(np.random.standard_normal((B, A, E)) * s_edge),
        "linear_w": bf(np.random.standard_normal((P, 2 * E)) / np.sqrt(2 * E) / s_cat * t[:, None]),
        "linear_b": bf(np.random.standard_normal(P) * 0.3 * t),
        "fwd_proj": bf(np.random.standard_normal((A, P, R)) / np.sqrt(P) / t[:, None]),
    }


def reference(image_features, edge_attributes, linear_w, linear_b, fwd_proj):
    w = f64(linear_w)
    node = mxq(f64(image_features), 1, "e4m3") @ mxq(w[:, :E].T, 0, "e4m3")
    edge = (mxq(f64(edge_attributes).reshape(B * A, E), 1, "e4m3") @ mxq(w[:, E:].T, 0, "e4m3")).reshape(B, A, P)
    agg = node[:, None, :] + edge + f64(linear_b)
    rep = mxq(agg.transpose(1, 0, 2), 2, "e4m3") @ mxq(f64(fwd_proj), 1, "e4m3")
    return rep.transpose(1, 0, 2)

@@ -1,0 +1,224 @@
+from contextlib import ExitStack
+
+import concourse.bass as bass
+import concourse.mybir as mybir
+import concourse.tile as tile
+from concourse.masks import make_identity
+
+F32 = mybir.dt.float32
+BF16 = mybir.dt.bfloat16
+U32 = mybir.dt.uint32
+U8 = mybir.dt.uint8
+FP8X4 = mybir.dt.float8_e4m3fn_x4
+ADD = mybir.AluOpType.add
+
+B, A, E, P, R = 1024, 8, 1024, 512, 256
+FLOPS = 2 * (B * E * P + B * A * E * P + B * A * P * R)
+
+MANUAL = True
+XBUFS = 6
+NT, NA, NO = 3, 3, 2
+REGROUP = {2: (("s", 0), ("s", 1)), 3: (("s", 2), ("s", 3)), 4: (("s", 4), ("s", 5)), 5: (("s", 6), ("s", 7))}
+QF = {4: 0, 6: 1}
+RSTART = 7
+RSLOTS = (0, 1, 2)
+
+
+def tile_attributegnn_pa_t_kernel(tc, image_features, edge_attributes, linear_w, linear_b, fwd_proj, out):
+    nc = tc.nc
+    w_v = linear_w.rearrange("(q t) (h k) -> h q t k", t=4, h=2)
+    img_v = image_features.rearrange("(c j) k -> c (j k)", j=8)
+    ea_v = edge_attributes.rearrange("(c j) a k -> c j (a k)", j=8)
+    f_v = fwd_proj.rearrange("a (q t) r -> q a (t r)", t=4)
+    out_v = out.rearrange("(c j) a r -> c j (a r)", j=8)
+    b_v = linear_b.rearrange("(q t) -> q t", t=4)
+
+    with ExitStack() as ctx:
+        const = ctx.enter_context(tc.tile_pool(name="const", bufs=1))
+        xpool = ctx.enter_context(tc.tile_pool(name="xpool", bufs=XBUFS))
+        gpool = ctx.enter_context(tc.tile_pool(name="gpool", bufs=3))
+        cpool = ctx.enter_context(tc.tile_pool(name="cpool", bufs=3))
+        apool = ctx.enter_context(tc.tile_pool(name="apool", bufs=3))
+        rpool = ctx.enter_context(tc.tile_pool(name="rpool", bufs=16))
+        opool = ctx.enter_context(tc.tile_pool(name="opool", bufs=3))
+        ps_t = ctx.enter_context(tc.psum_pool(name="ps_t", bufs=NT))
+        ps_a = ctx.enter_context(tc.psum_pool(name="ps_a", bufs=NA))
+        ps_o = ctx.enter_context(tc.psum_pool(name="ps_o", bufs=NO))
+        if MANUAL:
+            ctx.enter_context(tc.manual_schedule())
+
+        ident = const.tile([128, 128], F32, name="ident")
+        make_identity(nc, ident[:])
+        bias_bf = const.tile([128, 4], BF16, name="bias_bf")
+        with nc.allow_non_contiguous_dma(reason="512 bias values, four to a partition"):
+            nc.scalar.dma_start(out=bias_bf[:], in_=b_v)
+        bias32 = const.tile([128, 4], F32, name="bias32")
+        nc.vector.tensor_copy(out=bias32[:], in_=bias_bf[:])
+        nodeb = const.tile([128, 4096], F32, name="nodeb")
+        w_codes = [const.tile([128, 1024], U32, name="w_codes%d" % h, align_bytes=64) for h in range(2)]
+        w_scales = [const.tile([128, 1024], U8, name="w_scales%d" % h, align_bytes=64) for h in range(2)]
+        f_codes = const.tile([128, 2048], U32, name="f_codes", align_bytes=64)
+        f_scales = const.tile([128, 2048], U8, name="f_scales", align_bytes=64)
+        f_raw = [const.tile([128, 4096], BF16, name="f_raw%d" % h) for h in range(2)]
+        f_grp = [const.tile([128, 4096], BF16, name="f_grp%d" % h, align_bytes=64) for h in range(2)]
+
+        jobs = [("node", 0, 0)] + [("edge", u // 2, u % 2) for u in range(8)]
+        jobs = jobs + [("node", 1, 0)] + [("edge", u // 2, u % 2) for u in range(8, 16)]
+        njobs = len(jobs)
+
+        srcs = [("w", 0), ("job", 0), ("w", 1)] + [("job", i) for i in range(1, njobs)]
+        x_tiles = []
+
+        def load_next():
+            n = len(x_tiles)
+            if n >= len(srcs):
+                return
+            kind, idx = srcs[n]
+            x = xpool.tile([128, 4096], BF16, name="x", tag="x")
+            if kind == "w":
+                nc.sync.dma_start(out=x[:].rearrange("p (t k) -> p t k", t=4), in_=w_v[idx])
+            else:
+                jk, j0, j1 = jobs[idx]
+                if jk == "node":
+                    nc.sync.dma_start(out=x[:], in_=img_v[:, j0 * 4096:(j0 + 1) * 4096])
+                else:
+                    nc.sync.dma_start(out=x[:], in_=ea_v[:, j0, j1 * 4096:(j1 + 1) * 4096])
+            x_tiles.append(x)
+            if n == 4 or n == 5:
+                h = n - 4
+                nc.sync.dma_start(out=f_raw[h][:].rearrange("p (a s) -> p a s", a=4), in_=f_v[:, h * 4:(h + 1) * 4, :])
+
+        def transpose_unit(n):
+            x32 = x_tiles[n][:].bitcast(F32)
+            g = gpool.tile([128, 4096], BF16, name="g", tag="g", align_bytes=64)
+            g32 = g[:].bitcast(F32).rearrange("p (r g a c u) -> p r g a c u", r=2, g=2, a=2, c=128, u=2)
+            for aa in range(4):
+                xt = ps_t.tile([128, 512], F32, name="xt", tag="xt")
+                for s in range(4):
+                    col = aa * 512 + s * 128
+                    nc.tensor.transpose(xt[:, s * 128:(s + 1) * 128], x32[:, col:col + 128], ident[:])
+                nc.scalar.copy(out=g32[:, aa // 2, :, aa % 2, :, :],
+                               in_=xt[:].rearrange("p (g u c) -> p g c u", g=2, u=2, c=128))
+            load_next()
+            return g
+
+        def quantise_half(g, codes, scales, r):
+            nc.vector.quantize_mx(out=codes[:, r * 512:(r + 1) * 512].bitcast(FP8X4),
+                                  scales=scales[:, r * 512:(r + 1) * 512],
+                                  in_=g[:, r * 2048:(r + 1) * 2048])
+
+        def project(h, codes, scales, aa):
+            acc = ps_a.tile([128, 512], F32, name="acc", tag="acc")
+            for t in range(4):
+                for gi in range(2):
+                    wc = (t // 2) * 512 + gi * 256 + (t % 2) * 128
+                    dc = (aa // 2) * 512 + gi * 256 + (aa % 2) * 128
+                    nc.tensor.matmul_mx(out=acc[:, t * 128:(t + 1) * 128],
+                                        lhsT=w_codes[h][:, wc:wc + 128].bitcast(FP8X4),
+                                        lhsT_scale=w_scales[h][:, wc:wc + 128],
+                                        rhs=codes[:, dc:dc + 128].bitcast(FP8X4),
+                                        rhs_scale=scales[:, dc:dc + 128],
+                                        start=(gi == 0), stop=(gi == 1))
+            return acc
+
+        pending = []
+        done = [0]
+
+        o_tiles = {}
+
+        def rep_pair(now):
+            if done[0] >= len(pending):
+                return
+            a_codes, a_scales, born, j, half, r, last = pending[done[0]]
+            if born >= now:
+                return
+            done[0] += 1
+            if r == 0:
+                o_tiles[born] = opool.tile([128, 1024], F32, name="o_sb", tag="o_sb")
+            o_sb = o_tiles[born]
+            o = ps_o.tile([128, 512], F32, name="o", tag="o")
+            for s in range(2):
+                a = half * 4 + r * 2 + s
+                nc.tensor.matmul_mx(out=o[:, s * 256:(s + 1) * 256],
+                                    lhsT=a_codes[:, s * 128:(s + 1) * 128].bitcast(FP8X4),
+                                    lhsT_scale=a_scales[:, s * 128:(s + 1) * 128],
+                                    rhs=f_codes[:, a * 256:(a + 1) * 256].bitcast(FP8X4),
+                                    rhs_scale=f_scales[:, a * 256:(a + 1) * 256],
+                                    start=True, stop=True)
+            nc.scalar.copy(out=o_sb[:, r * 512:(r + 1) * 512], in_=o[:])
+            if last:
+                c0 = half * 1024 + r * 512
+                nc.scalar.dma_start(out=out_v[:, j, c0:c0 + 512], in_=o_sb[:, r * 512:(r + 1) * 512])
+            elif r == 1:
+                nc.scalar.dma_start(out=out_v[:, j, half * 1024:(half + 1) * 1024], in_=o_sb[:])
+
+        def regroup(eng, a):
+            src = f_raw[a // 4][:, (a % 4) * 1024:(a % 4 + 1) * 1024].rearrange("p (t c i) -> p c t i", t=4, i=4)
+            dst = f_grp[a // 4][:, (a % 4) * 1024:(a % 4 + 1) * 1024].rearrange("p (c i t) -> p c t i", t=4, i=4)
+            if eng == "s":
+                nc.scalar.copy(out=dst, in_=src)
+            else:
+                nc.vector.tensor_copy(out=dst, in_=src)
+
+        for n in range(XBUFS):
+            load_next()
+
+        g = transpose_unit(0)
+        for r in range(2):
+            quantise_half(g, w_codes[0], w_scales[0], r)
+        g_job = transpose_unit(1)
+        codes = cpool.tile([128, 1024], U32, name="codes", tag="codes", align_bytes=64)
+        scales = cpool.tile([128, 1024], U8, name="scales", tag="scales", align_bytes=64)
+        for r in range(2):
+            quantise_half(g_job, codes, scales, r)
+        g = transpose_unit(2)
+        for r in range(2):
+            quantise_half(g, w_codes[1], w_scales[1], r)
+
+        for i in range(njobs):
+            kind, j0, j1 = jobs[i]
+            if i + 1 < njobs:
+                g_next = transpose_unit(i + 3)
+                codes_next = cpool.tile([128, 1024], U32, name="codes", tag="codes", align_bytes=64)
+                scales_next = cpool.tile([128, 1024], U8, name="scales", tag="scales", align_bytes=64)
+            extra = list(REGROUP.get(i, ()))
+            if kind == "edge":
+                agg = apool.tile([128, 2048], BF16, name="agg", tag="agg", align_bytes=64)
+            for aa in range(4):
+                acc = project(0 if kind == "node" else 1, codes, scales, aa)
+                acc_v = acc[:].rearrange("p (t c) -> p c t", t=4)
+                if kind == "node":
+                    j = j0 * 4 + aa
+                    nc.vector.tensor_tensor(out=nodeb[:, j * 512:(j + 1) * 512].rearrange("p (c t) -> p c t", t=4),
+                                            in0=acc_v, in1=bias32[:].unsqueeze(1).to_broadcast([128, 128, 4]), op=ADD)
+                else:
+                    nc.vector.tensor_tensor(out=agg[:, aa * 512:(aa + 1) * 512].rearrange("p (c t) -> p c t", t=4),
+                                            in0=acc_v,
+                                            in1=nodeb[:, j0 * 512:(j0 + 1) * 512].rearrange("p (c t) -> p c t", t=4),
+                                            op=ADD)
+                if aa % 2 == 0 and len(extra) > aa // 2:
+                    regroup(extra[aa // 2][0], extra[aa // 2][1])
+                if aa == 1 and i + 1 < njobs:
+                    quantise_half(g_next, codes_next, scales_next, 0)
+                if aa == 3 and i + 1 < njobs:
+                    quantise_half(g_next, codes_next, scales_next, 1)
+                if kind == "edge" and aa >= 2:
+                    r = aa - 2
+                    a_codes = rpool.tile([128, 256], U32, name="a_codes", tag="a_codes", align_bytes=64)
+                    a_scales = rpool.tile([128, 256], U8, name="a_scales", tag="a_scales", align_bytes=64)
+                    nc.vector.quantize_mx(out=a_codes[:].bitcast(FP8X4), scales=a_scales[:],
+                                          in_=agg[:, r * 1024:(r + 1) * 1024])
+                    pending.append((a_codes, a_scales, i, j0, j1, r, i == njobs - 1))
+                if aa == 3 and i in QF:
+                    h = QF[i]
+                    for r in range(2):
+                        c0 = h * 1024 + r * 512
+                        nc.vector.quantize_mx(out=f_codes[:, c0:c0 + 512].bitcast(FP8X4),
+                                              scales=f_scales[:, c0:c0 + 512],
+                                              in_=f_grp[h][:, r * 2048:(r + 1) * 2048])
+                if i >= RSTART and aa in RSLOTS:
+                    rep_pair(i)
+            if i + 1 < njobs:
+                codes, scales = codes_next, scales_next
+        for n in range(len(pending) - done[0]):
+            rep_pair(njobs)

@@ -17,7 +17,6 @@ FLOPS = 2 * (B * E * P + B * A * E * P + B * A * P * R)
 
 MANUAL = True
 XBUFS = 6
-NT, NA, NO = 3, 3, 2
 REGROUP = {2: (("s", 0), ("s", 1)), 3: (("s", 2), ("s", 3)), 4: (("s", 4), ("s", 5)), 5: (("s", 6), ("s", 7))}
 QF = {4: 0, 6: 1}
 RSTART = 7
@@ -41,11 +40,16 @@ def tile_attributegnn_pa_t_kernel(tc, image_features, edge_attributes, linear_w,
         apool = ctx.enter_context(tc.tile_pool(name="apool", bufs=3))
         rpool = ctx.enter_context(tc.tile_pool(name="rpool", bufs=16))
         opool = ctx.enter_context(tc.tile_pool(name="opool", bufs=3))
-        ps_t = ctx.enter_context(tc.psum_pool(name="ps_t", bufs=NT))
-        ps_a = ctx.enter_context(tc.psum_pool(name="ps_a", bufs=NA))
-        ps_o = ctx.enter_context(tc.psum_pool(name="ps_o", bufs=NO))
+        psum = ctx.enter_context(tc.psum_pool(name="psum", bufs=1))
         if MANUAL:
             ctx.enter_context(tc.manual_schedule())
+
+        banks_used = [0]
+
+        def next_bank():
+            k = banks_used[0] % 8
+            banks_used[0] += 1
+            return psum.tile([128, 512], F32, name="bank%d" % k, tag="bank%d" % k)
 
         ident = const.tile([128, 128], F32, name="ident")
         make_identity(nc, ident[:])
@@ -93,7 +97,7 @@ def tile_attributegnn_pa_t_kernel(tc, image_features, edge_attributes, linear_w,
             g = gpool.tile([128, 4096], BF16, name="g", tag="g", align_bytes=64)
             g32 = g[:].bitcast(F32).rearrange("p (r g a c u) -> p r g a c u", r=2, g=2, a=2, c=128, u=2)
             for aa in range(4):
-                xt = ps_t.tile([128, 512], F32, name="xt", tag="xt")
+                xt = next_bank()
                 for s in range(4):
                     col = aa * 512 + s * 128
                     nc.tensor.transpose(xt[:, s * 128:(s + 1) * 128], x32[:, col:col + 128], ident[:])
@@ -108,7 +112,7 @@ def tile_attributegnn_pa_t_kernel(tc, image_features, edge_attributes, linear_w,
                                   in_=g[:, r * 2048:(r + 1) * 2048])
 
         def project(h, codes, scales, aa):
-            acc = ps_a.tile([128, 512], F32, name="acc", tag="acc")
+            acc = next_bank()
             for t in range(4):
                 for gi in range(2):
                     wc = (t // 2) * 512 + gi * 256 + (t % 2) * 128
@@ -136,7 +140,7 @@ def tile_attributegnn_pa_t_kernel(tc, image_features, edge_attributes, linear_w,
             if r == 0:
                 o_tiles[born] = opool.tile([128, 1024], F32, name="o_sb", tag="o_sb")
             o_sb = o_tiles[born]
-            o = ps_o.tile([128, 512], F32, name="o", tag="o")
+            o = next_bank()
             for s in range(2):
                 a = half * 4 + r * 2 + s
                 nc.tensor.matmul_mx(out=o[:, s * 256:(s + 1) * 256],

@@ -21,6 +21,7 @@ REGROUP = {2: (("s", 0), ("s", 1)), 3: (("s", 2), ("s", 3)), 4: (("s", 4), ("s",
 QF = {4: 0, 6: 1}
 RSTART = 7
 RSLOTS = (0, 1, 2)
+LATE_SLOTS = (1, 2, 3)
 
 
 def tile_attributegnn_pa_t_kernel(tc, image_features, edge_attributes, linear_w, linear_b, fwd_proj, out):
@@ -80,10 +81,15 @@ def tile_attributegnn_pa_t_kernel(tc, image_features, edge_attributes, linear_w,
             kind, idx = srcs[n]
             x = xpool.tile([128, 4096], BF16, name="x", tag="x")
             if kind == "w":
-                nc.sync.dma_start(out=x[:].rearrange("p (t k) -> p t k", t=4), in_=w_v[idx])
+                for t in range(4):
+                    nc.sync.dma_start(out=x[:, t * 1024:(t + 1) * 1024], in_=w_v[idx][:, t, :])
             else:
                 jk, j0, j1 = jobs[idx]
-                if jk == "node":
+                if jk == "node" and n < 3:
+                    for t in range(4):
+                        c0 = j0 * 4096 + t * 1024
+                        nc.sync.dma_start(out=x[:, t * 1024:(t + 1) * 1024], in_=img_v[:, c0:c0 + 1024])
+                elif jk == "node":
                     nc.sync.dma_start(out=x[:], in_=img_v[:, j0 * 4096:(j0 + 1) * 4096])
                 else:
                     nc.sync.dma_start(out=x[:], in_=ea_v[:, j0, j1 * 4096:(j1 + 1) * 4096])
@@ -133,28 +139,36 @@ def tile_attributegnn_pa_t_kernel(tc, image_features, edge_attributes, linear_w,
         def rep_pair(now):
             if done[0] >= len(pending):
                 return
-            a_codes, a_scales, born, j, half, r, last = pending[done[0]]
+            a_codes, a_scales, born, j, half, a0, na, last = pending[done[0]]
             if born >= now:
                 return
             done[0] += 1
-            if r == 0:
+            if a0 == 0:
                 o_tiles[born] = opool.tile([128, 1024], F32, name="o_sb", tag="o_sb")
             o_sb = o_tiles[born]
             o = next_bank()
-            for s in range(2):
-                a = half * 4 + r * 2 + s
+            for s in range(na):
+                a = half * 4 + a0 + s
                 nc.tensor.matmul_mx(out=o[:, s * 256:(s + 1) * 256],
                                     lhsT=a_codes[:, s * 128:(s + 1) * 128].bitcast(FP8X4),
                                     lhsT_scale=a_scales[:, s * 128:(s + 1) * 128],
                                     rhs=f_codes[:, a * 256:(a + 1) * 256].bitcast(FP8X4),
                                     rhs_scale=f_scales[:, a * 256:(a + 1) * 256],
                                     start=True, stop=True)
-            nc.scalar.copy(out=o_sb[:, r * 512:(r + 1) * 512], in_=o[:])
+            nc.scalar.copy(out=o_sb[:, a0 * 256:(a0 + na) * 256], in_=o[:, 0:na * 256])
             if last:
-                c0 = half * 1024 + r * 512
-                nc.scalar.dma_start(out=out_v[:, j, c0:c0 + 512], in_=o_sb[:, r * 512:(r + 1) * 512])
-            elif r == 1:
+                c0 = half * 1024 + a0 * 256
+                nc.scalar.dma_start(out=out_v[:, j, c0:c0 + na * 256], in_=o_sb[:, a0 * 256:(a0 + na) * 256])
+            elif a0 + na == 4:
                 nc.scalar.dma_start(out=out_v[:, j, half * 1024:(half + 1) * 1024], in_=o_sb[:])
+
+        def quantise_agg(agg, i, a0, na):
+            kind, j0, j1 = jobs[i]
+            a_codes = rpool.tile([128, 256], U32, name="a_codes", tag="a_codes", align_bytes=64)
+            a_scales = rpool.tile([128, 256], U8, name="a_scales", tag="a_scales", align_bytes=64)
+            nc.vector.quantize_mx(out=a_codes[:, 0:na * 128].bitcast(FP8X4), scales=a_scales[:, 0:na * 128],
+                                  in_=agg[:, a0 * 512:(a0 + na) * 512])
+            pending.append((a_codes, a_scales, i, j0, j1, a0, na, i == njobs - 1))
 
         def regroup(eng, a):
             src = f_raw[a // 4][:, (a % 4) * 1024:(a % 4 + 1) * 1024].rearrange("p (t c i) -> p c t i", t=4, i=4)
@@ -181,7 +195,7 @@ def tile_attributegnn_pa_t_kernel(tc, image_features, edge_attributes, linear_w,
 
         for i in range(njobs):
             kind, j0, j1 = jobs[i]
-            if i + 1 < njobs:
+            if i + 1 < njobs and i > 0:
                 g_next = transpose_unit(i + 3)
                 codes_next = cpool.tile([128, 1024], U32, name="codes", tag="codes", align_bytes=64)
                 scales_next = cpool.tile([128, 1024], U8, name="scales", tag="scales", align_bytes=64)
@@ -202,17 +216,17 @@ def tile_attributegnn_pa_t_kernel(tc, image_features, edge_attributes, linear_w,
                                             op=ADD)
                 if aa % 2 == 0 and len(extra) > aa // 2:
                     regroup(extra[aa // 2][0], extra[aa // 2][1])
-                if aa == 1 and i + 1 < njobs:
+                if aa == 1 and i + 1 < njobs and i > 0:
                     quantise_half(g_next, codes_next, scales_next, 0)
-                if aa == 3 and i + 1 < njobs:
+                if aa == 3 and i + 1 < njobs and i > 0:
                     quantise_half(g_next, codes_next, scales_next, 1)
-                if kind == "edge" and aa >= 2:
-                    r = aa - 2
-                    a_codes = rpool.tile([128, 256], U32, name="a_codes", tag="a_codes", align_bytes=64)
-                    a_scales = rpool.tile([128, 256], U8, name="a_scales", tag="a_scales", align_bytes=64)
-                    nc.vector.quantize_mx(out=a_codes[:].bitcast(FP8X4), scales=a_scales[:],
-                                          in_=agg[:, r * 1024:(r + 1) * 1024])
-                    pending.append((a_codes, a_scales, i, j0, j1, r, i == njobs - 1))
+                if kind == "edge" and i == njobs - 1:
+                    if aa == 1:
+                        quantise_agg(agg, i, 0, 2)
+                    elif aa >= 2:
+                        quantise_agg(agg, i, aa, 1)
+                elif kind == "edge" and aa >= 2:
+                    quantise_agg(agg, i, (aa - 2) * 2, 2)
                 if aa == 3 and i in QF:
                     h = QF[i]
                     for r in range(2):
@@ -220,8 +234,14 @@ def tile_attributegnn_pa_t_kernel(tc, image_features, edge_attributes, linear_w,
                         nc.vector.quantize_mx(out=f_codes[:, c0:c0 + 512].bitcast(FP8X4),
                                               scales=f_scales[:, c0:c0 + 512],
                                               in_=f_grp[h][:, r * 2048:(r + 1) * 2048])
-                if i >= RSTART and aa in RSLOTS:
+                if i >= RSTART and aa in (LATE_SLOTS if i >= njobs - 2 else RSLOTS):
                     rep_pair(i)
+            if i == 0:
+                g_next = transpose_unit(3)
+                codes_next = cpool.tile([128, 1024], U32, name="codes", tag="codes", align_bytes=64)
+                scales_next = cpool.tile([128, 1024], U8, name="scales", tag="scales", align_bytes=64)
+                for r in range(2):
+                    quantise_half(g_next, codes_next, scales_next, r)
             if i + 1 < njobs:
                 codes, scales = codes_next, scales_next
         for n in range(len(pending) - done[0]):

@@ -158,9 +158,9 @@ def tile_attributegnn_pa_t_kernel(tc, image_features, edge_attributes, linear_w,
             nc.scalar.copy(out=o_sb[:, a0 * 256:(a0 + na) * 256], in_=o[:, 0:na * 256])
             if last:
                 c0 = half * 1024 + a0 * 256
-                nc.scalar.dma_start(out=out_v[:, j, c0:c0 + na * 256], in_=o_sb[:, a0 * 256:(a0 + na) * 256])
+                nc.sync.dma_start(out=out_v[:, j, c0:c0 + na * 256], in_=o_sb[:, a0 * 256:(a0 + na) * 256])
             elif a0 + na == 4:
-                nc.scalar.dma_start(out=out_v[:, j, half * 1024:(half + 1) * 1024], in_=o_sb[:])
+                nc.sync.dma_start(out=out_v[:, j, half * 1024:(half + 1) * 1024], in_=o_sb[:])
 
         def quantise_agg(agg, i, a0, na):
             kind, j0, j1 = jobs[i]

@@ -1,8 +1,6 @@
 from contextlib import ExitStack
 
-import concourse.bass as bass
 import concourse.mybir as mybir
-import concourse.tile as tile
 from concourse.masks import make_identity
 
 F32 = mybir.dt.float32
@@ -12,237 +10,258 @@ U8 = mybir.dt.uint8
 FP8X4 = mybir.dt.float8_e4m3fn_x4
 ADD = mybir.AluOpType.add
 
-B, A, E, P, R = 1024, 8, 1024, 512, 256
-FLOPS = 2 * (B * E * P + B * A * E * P + B * A * P * R)
+NODES, ATTRS, FEATS, PROJ, REP = 1024, 8, 1024, 512, 256
+FLOPS = 2 * (NODES * FEATS * PROJ + NODES * ATTRS * FEATS * PROJ + NODES * ATTRS * PROJ * REP)
 
-MANUAL = True
-XBUFS = 6
-REGROUP = {2: (("s", 0), ("s", 1)), 3: (("s", 2), ("s", 3)), 4: (("s", 4), ("s", 5)), 5: (("s", 6), ("s", 7))}
-QF = {4: 0, 6: 1}
-RSTART = 7
-RSLOTS = (0, 1, 2)
-LATE_SLOTS = (1, 2, 3)
+P = 128
+STRIPS = 4
+SLAB = STRIPS * FEATS
+BANK = 512
+N_BANKS = 8
+BLOCKS = NODES // P
+HALF = SLAB // 2
+
+SLABS_AHEAD = 6
+FWD_LOADED_BEHIND = (4, 5)
+FWD_REGROUP_FROM = 2
+FWD_QUANTISED_AFTER = {4: 0, 6: 1}
+OUT_FROM = 9
+GROUPS_OF_TWO_FROM = 6
+OUT_BEHIND_STRIPS = (0, 1, 2)
+OUT_BEHIND_STRIPS_AT_END = (1, 2, 3)
 
 
 def tile_attributegnn_pa_t_kernel(tc, image_features, edge_attributes, linear_w, linear_b, fwd_proj, out):
     nc = tc.nc
-    w_v = linear_w.rearrange("(q t) (h k) -> h q t k", t=4, h=2)
-    img_v = image_features.rearrange("(c j) k -> c (j k)", j=8)
-    ea_v = edge_attributes.rearrange("(c j) a k -> c j (a k)", j=8)
+    w_v = linear_w.rearrange("(q t) (h k) -> h q t k", t=STRIPS, h=2)
+    img_v = image_features.rearrange("(c j) k -> c (j k)", j=BLOCKS)
+    ea_v = edge_attributes.rearrange("(c j) a k -> c j (a k)", j=BLOCKS)
     f_v = fwd_proj.rearrange("a (q t) r -> q a (t r)", t=4)
-    out_v = out.rearrange("(c j) a r -> c j (a r)", j=8)
+    out_v = out.rearrange("(c j) a r -> c j (a r)", j=BLOCKS)
     b_v = linear_b.rearrange("(q t) -> q t", t=4)
+
+    edge_jobs = [("edge", u // 2, u % 2) for u in range(2 * BLOCKS)]
+    jobs = [("node", 0, 0)] + edge_jobs[:BLOCKS] + [("node", 1, 0)] + edge_jobs[BLOCKS:]
+    last_job = len(jobs) - 1
+    slabs = [("w", 0), ("job", 0), ("w", 1)] + [("job", i) for i in range(1, len(jobs))]
 
     with ExitStack() as ctx:
         const = ctx.enter_context(tc.tile_pool(name="const", bufs=1))
-        xpool = ctx.enter_context(tc.tile_pool(name="xpool", bufs=XBUFS))
-        gpool = ctx.enter_context(tc.tile_pool(name="gpool", bufs=3))
-        cpool = ctx.enter_context(tc.tile_pool(name="cpool", bufs=3))
+        xpool = ctx.enter_context(tc.tile_pool(name="xpool", bufs=SLABS_AHEAD))
+        gpool = ctx.enter_context(tc.tile_pool(name="gpool", bufs=4))
+        cpool = ctx.enter_context(tc.tile_pool(name="cpool", bufs=5))
         apool = ctx.enter_context(tc.tile_pool(name="apool", bufs=3))
-        rpool = ctx.enter_context(tc.tile_pool(name="rpool", bufs=16))
+        rpool = ctx.enter_context(tc.tile_pool(name="rpool", bufs=20))
         opool = ctx.enter_context(tc.tile_pool(name="opool", bufs=3))
         psum = ctx.enter_context(tc.psum_pool(name="psum", bufs=1))
-        if MANUAL:
-            ctx.enter_context(tc.manual_schedule())
+        ctx.enter_context(tc.manual_schedule())
 
         banks_used = [0]
 
         def next_bank():
-            k = banks_used[0] % 8
+            k = banks_used[0] % N_BANKS
             banks_used[0] += 1
-            return psum.tile([128, 512], F32, name="bank%d" % k, tag="bank%d" % k)
+            return psum.tile([P, BANK], F32, name="bank%d" % k, tag="bank%d" % k)
 
-        ident = const.tile([128, 128], F32, name="ident")
+        ident = const.tile([P, P], F32, name="ident")
         make_identity(nc, ident[:])
-        bias_bf = const.tile([128, 4], BF16, name="bias_bf")
+        bias_bf = const.tile([P, 4], BF16, name="bias_bf")
         with nc.allow_non_contiguous_dma(reason="512 bias values, four to a partition"):
             nc.scalar.dma_start(out=bias_bf[:], in_=b_v)
-        bias32 = const.tile([128, 4], F32, name="bias32")
+        bias32 = const.tile([P, 4], F32, name="bias32")
         nc.vector.tensor_copy(out=bias32[:], in_=bias_bf[:])
-        nodeb = const.tile([128, 4096], F32, name="nodeb")
-        w_codes = [const.tile([128, 1024], U32, name="w_codes%d" % h, align_bytes=64) for h in range(2)]
-        w_scales = [const.tile([128, 1024], U8, name="w_scales%d" % h, align_bytes=64) for h in range(2)]
-        f_codes = const.tile([128, 2048], U32, name="f_codes", align_bytes=64)
-        f_scales = const.tile([128, 2048], U8, name="f_scales", align_bytes=64)
-        f_raw = [const.tile([128, 4096], BF16, name="f_raw%d" % h) for h in range(2)]
-        f_grp = [const.tile([128, 4096], BF16, name="f_grp%d" % h, align_bytes=64) for h in range(2)]
+        nodeb = const.tile([P, BLOCKS * BANK], F32, name="nodeb")
+        w_codes = [const.tile([P, SLAB // 4], U32, name="w_codes%d" % h, align_bytes=64) for h in range(2)]
+        w_scales = [const.tile([P, SLAB // 4], U8, name="w_scales%d" % h, align_bytes=64) for h in range(2)]
+        f_codes = const.tile([P, ATTRS * REP], U32, name="f_codes", align_bytes=64)
+        f_scales = const.tile([P, ATTRS * REP], U8, name="f_scales", align_bytes=64)
+        f_raw = [const.tile([P, 4 * 4 * REP], BF16, name="f_raw%d" % h) for h in range(2)]
+        f_grp = [const.tile([P, 4 * 4 * REP], BF16, name="f_grp%d" % h, align_bytes=64) for h in range(2)]
 
-        jobs = [("node", 0, 0)] + [("edge", u // 2, u % 2) for u in range(8)]
-        jobs = jobs + [("node", 1, 0)] + [("edge", u // 2, u % 2) for u in range(8, 16)]
-        njobs = len(jobs)
-
-        srcs = [("w", 0), ("job", 0), ("w", 1)] + [("job", i) for i in range(1, njobs)]
         x_tiles = []
 
-        def load_next():
+        def load_next_slab():
             n = len(x_tiles)
-            if n >= len(srcs):
+            if n >= len(slabs):
                 return
-            kind, idx = srcs[n]
-            x = xpool.tile([128, 4096], BF16, name="x", tag="x")
+            kind, idx = slabs[n]
+            x = xpool.tile([P, SLAB], BF16, name="x", tag="x")
             if kind == "w":
-                for t in range(4):
-                    nc.sync.dma_start(out=x[:, t * 1024:(t + 1) * 1024], in_=w_v[idx][:, t, :])
+                for t in range(STRIPS):
+                    nc.sync.dma_start(out=x[:, t * FEATS:(t + 1) * FEATS], in_=w_v[idx][:, t, :])
             else:
-                jk, j0, j1 = jobs[idx]
-                if jk == "node" and n < 3:
-                    for t in range(4):
-                        c0 = j0 * 4096 + t * 1024
-                        nc.sync.dma_start(out=x[:, t * 1024:(t + 1) * 1024], in_=img_v[:, c0:c0 + 1024])
-                elif jk == "node":
-                    nc.sync.dma_start(out=x[:], in_=img_v[:, j0 * 4096:(j0 + 1) * 4096])
+                job_kind, j0, j1 = jobs[idx]
+                if job_kind == "node" and idx == 0:
+                    for t in range(STRIPS):
+                        c0 = j0 * SLAB + t * FEATS
+                        nc.sync.dma_start(out=x[:, t * FEATS:(t + 1) * FEATS], in_=img_v[:, c0:c0 + FEATS])
+                elif job_kind == "node":
+                    nc.sync.dma_start(out=x[:], in_=img_v[:, j0 * SLAB:(j0 + 1) * SLAB])
                 else:
-                    nc.sync.dma_start(out=x[:], in_=ea_v[:, j0, j1 * 4096:(j1 + 1) * 4096])
+                    nc.sync.dma_start(out=x[:], in_=ea_v[:, j0, j1 * SLAB:(j1 + 1) * SLAB])
             x_tiles.append(x)
-            if n == 4 or n == 5:
-                h = n - 4
+            if n in FWD_LOADED_BEHIND:
+                h = FWD_LOADED_BEHIND.index(n)
                 nc.sync.dma_start(out=f_raw[h][:].rearrange("p (a s) -> p a s", a=4), in_=f_v[:, h * 4:(h + 1) * 4, :])
 
-        def transpose_unit(n):
+        def transpose_slab(n):
             x32 = x_tiles[n][:].bitcast(F32)
-            g = gpool.tile([128, 4096], BF16, name="g", tag="g", align_bytes=64)
-            g32 = g[:].bitcast(F32).rearrange("p (r g a c u) -> p r g a c u", r=2, g=2, a=2, c=128, u=2)
-            for aa in range(4):
+            g = gpool.tile([P, SLAB], BF16, name="g", tag="g", align_bytes=64)
+            g32 = g[:].bitcast(F32).rearrange("p (r g a c u) -> p r g a c u", r=2, g=2, a=2, c=P, u=2)
+            for s in range(STRIPS):
                 xt = next_bank()
-                for s in range(4):
-                    col = aa * 512 + s * 128
-                    nc.tensor.transpose(xt[:, s * 128:(s + 1) * 128], x32[:, col:col + 128], ident[:])
-                nc.scalar.copy(out=g32[:, aa // 2, :, aa % 2, :, :],
-                               in_=xt[:].rearrange("p (g u c) -> p g c u", g=2, u=2, c=128))
-            load_next()
+                for piece in range(4):
+                    col = s * (FEATS // 2) + piece * P
+                    nc.tensor.transpose(xt[:, piece * P:(piece + 1) * P], x32[:, col:col + P], ident[:])
+                nc.scalar.copy(out=g32[:, s // 2, :, s % 2, :, :],
+                               in_=xt[:].rearrange("p (g u c) -> p g c u", g=2, u=2, c=P))
+            load_next_slab()
             return g
 
-        def quantise_half(g, codes, scales, r):
-            nc.vector.quantize_mx(out=codes[:, r * 512:(r + 1) * 512].bitcast(FP8X4),
-                                  scales=scales[:, r * 512:(r + 1) * 512],
-                                  in_=g[:, r * 2048:(r + 1) * 2048])
+        def quantise_pair_of_strips(g, codes, scales, r):
+            nc.vector.quantize_mx(out=codes[:, r * (HALF // 4):(r + 1) * (HALF // 4)].bitcast(FP8X4),
+                                  scales=scales[:, r * (HALF // 4):(r + 1) * (HALF // 4)],
+                                  in_=g[:, r * HALF:(r + 1) * HALF])
 
-        def project(h, codes, scales, aa):
+        def new_codes():
+            codes = cpool.tile([P, SLAB // 4], U32, name="codes", tag="codes", align_bytes=64)
+            scales = cpool.tile([P, SLAB // 4], U8, name="scales", tag="scales", align_bytes=64)
+            return codes, scales
+
+        def words_of(s, g):
+            return (s // 2) * 512 + g * 256 + (s % 2) * P
+
+        def project(h, codes, scales, s):
             acc = next_bank()
-            for t in range(4):
-                for gi in range(2):
-                    wc = (t // 2) * 512 + gi * 256 + (t % 2) * 128
-                    dc = (aa // 2) * 512 + gi * 256 + (aa % 2) * 128
-                    nc.tensor.matmul_mx(out=acc[:, t * 128:(t + 1) * 128],
-                                        lhsT=w_codes[h][:, wc:wc + 128].bitcast(FP8X4),
-                                        lhsT_scale=w_scales[h][:, wc:wc + 128],
-                                        rhs=codes[:, dc:dc + 128].bitcast(FP8X4),
-                                        rhs_scale=scales[:, dc:dc + 128],
-                                        start=(gi == 0), stop=(gi == 1))
+            for t in range(STRIPS):
+                for g in range(2):
+                    wc = words_of(t, g)
+                    dc = words_of(s, g)
+                    nc.tensor.matmul_mx(out=acc[:, t * P:(t + 1) * P],
+                                        lhsT=w_codes[h][:, wc:wc + P].bitcast(FP8X4),
+                                        lhsT_scale=w_scales[h][:, wc:wc + P],
+                                        rhs=codes[:, dc:dc + P].bitcast(FP8X4),
+                                        rhs_scale=scales[:, dc:dc + P],
+                                        start=(g == 0), stop=(g == 1))
             return acc
 
-        pending = []
-        done = [0]
-
+        waiting = []
+        taken = [0]
         o_tiles = {}
 
-        def rep_pair(now):
-            if done[0] >= len(pending):
+        def quantise_agg(agg, i, s0, n_strips):
+            job_kind, j0, j1 = jobs[i]
+            a_codes = rpool.tile([P, 2 * P], U32, name="a_codes", tag="a_codes", align_bytes=64)
+            a_scales = rpool.tile([P, 2 * P], U8, name="a_scales", tag="a_scales", align_bytes=64)
+            nc.vector.quantize_mx(out=a_codes[:, 0:n_strips * P].bitcast(FP8X4), scales=a_scales[:, 0:n_strips * P],
+                                  in_=agg[:, s0 * BANK:(s0 + n_strips) * BANK])
+            waiting.append((a_codes, a_scales, i, j0, j1, s0, n_strips))
+
+        def second_product(now):
+            if taken[0] >= len(waiting):
                 return
-            a_codes, a_scales, born, j, half, a0, na, last = pending[done[0]]
-            if born >= now:
+            a_codes, a_scales, i, j, half, s0, n_strips = waiting[taken[0]]
+            if i >= now:
                 return
-            done[0] += 1
-            if a0 == 0:
-                o_tiles[born] = opool.tile([128, 1024], F32, name="o_sb", tag="o_sb")
-            o_sb = o_tiles[born]
+            taken[0] += 1
+            if s0 == 0:
+                o_tiles[i] = opool.tile([P, STRIPS * REP], F32, name="o_sb", tag="o_sb")
+            o_sb = o_tiles[i]
             o = next_bank()
-            for s in range(na):
-                a = half * 4 + a0 + s
-                nc.tensor.matmul_mx(out=o[:, s * 256:(s + 1) * 256],
-                                    lhsT=a_codes[:, s * 128:(s + 1) * 128].bitcast(FP8X4),
-                                    lhsT_scale=a_scales[:, s * 128:(s + 1) * 128],
-                                    rhs=f_codes[:, a * 256:(a + 1) * 256].bitcast(FP8X4),
-                                    rhs_scale=f_scales[:, a * 256:(a + 1) * 256],
+            for s in range(n_strips):
+                a = half * STRIPS + s0 + s
+                nc.tensor.matmul_mx(out=o[:, s * REP:(s + 1) * REP],
+                                    lhsT=a_codes[:, s * P:(s + 1) * P].bitcast(FP8X4),
+                                    lhsT_scale=a_scales[:, s * P:(s + 1) * P],
+                                    rhs=f_codes[:, a * REP:(a + 1) * REP].bitcast(FP8X4),
+                                    rhs_scale=f_scales[:, a * REP:(a + 1) * REP],
                                     start=True, stop=True)
-            nc.scalar.copy(out=o_sb[:, a0 * 256:(a0 + na) * 256], in_=o[:, 0:na * 256])
-            if last:
-                c0 = half * 1024 + a0 * 256
-                nc.sync.dma_start(out=out_v[:, j, c0:c0 + na * 256], in_=o_sb[:, a0 * 256:(a0 + na) * 256])
-            elif a0 + na == 4:
-                nc.sync.dma_start(out=out_v[:, j, half * 1024:(half + 1) * 1024], in_=o_sb[:])
+            nc.scalar.copy(out=o_sb[:, s0 * REP:(s0 + n_strips) * REP], in_=o[:, 0:n_strips * REP])
+            if i == last_job:
+                c0 = (half * STRIPS + s0) * REP
+                nc.scalar.dma_start(out=out_v[:, j, c0:c0 + n_strips * REP],
+                                    in_=o_sb[:, s0 * REP:(s0 + n_strips) * REP])
+            elif s0 + n_strips == STRIPS:
+                nc.scalar.dma_start(out=out_v[:, j, half * STRIPS * REP:(half + 1) * STRIPS * REP], in_=o_sb[:])
 
-        def quantise_agg(agg, i, a0, na):
-            kind, j0, j1 = jobs[i]
-            a_codes = rpool.tile([128, 256], U32, name="a_codes", tag="a_codes", align_bytes=64)
-            a_scales = rpool.tile([128, 256], U8, name="a_scales", tag="a_scales", align_bytes=64)
-            nc.vector.quantize_mx(out=a_codes[:, 0:na * 128].bitcast(FP8X4), scales=a_scales[:, 0:na * 128],
-                                  in_=agg[:, a0 * 512:(a0 + na) * 512])
-            pending.append((a_codes, a_scales, i, j0, j1, a0, na, i == njobs - 1))
+        def regroup_fwd(a):
+            cols = slice((a % 4) * 4 * REP, (a % 4 + 1) * 4 * REP)
+            nc.scalar.copy(out=f_grp[a // 4][:, cols].rearrange("p (c i t) -> p c t i", t=4, i=4),
+                           in_=f_raw[a // 4][:, cols].rearrange("p (t c i) -> p c t i", t=4, i=4))
 
-        def regroup(eng, a):
-            src = f_raw[a // 4][:, (a % 4) * 1024:(a % 4 + 1) * 1024].rearrange("p (t c i) -> p c t i", t=4, i=4)
-            dst = f_grp[a // 4][:, (a % 4) * 1024:(a % 4 + 1) * 1024].rearrange("p (c i t) -> p c t i", t=4, i=4)
-            if eng == "s":
-                nc.scalar.copy(out=dst, in_=src)
-            else:
-                nc.vector.tensor_copy(out=dst, in_=src)
+        for n in range(SLABS_AHEAD):
+            load_next_slab()
 
-        for n in range(XBUFS):
-            load_next()
-
-        g = transpose_unit(0)
+        g = transpose_slab(0)
         for r in range(2):
-            quantise_half(g, w_codes[0], w_scales[0], r)
-        g_job = transpose_unit(1)
-        codes = cpool.tile([128, 1024], U32, name="codes", tag="codes", align_bytes=64)
-        scales = cpool.tile([128, 1024], U8, name="scales", tag="scales", align_bytes=64)
+            quantise_pair_of_strips(g, w_codes[0], w_scales[0], r)
+        g = transpose_slab(1)
+        codes, scales = new_codes()
         for r in range(2):
-            quantise_half(g_job, codes, scales, r)
-        g = transpose_unit(2)
+            quantise_pair_of_strips(g, codes, scales, r)
+        g = transpose_slab(2)
         for r in range(2):
-            quantise_half(g, w_codes[1], w_scales[1], r)
+            quantise_pair_of_strips(g, w_codes[1], w_scales[1], r)
 
-        for i in range(njobs):
-            kind, j0, j1 = jobs[i]
-            if i + 1 < njobs and i > 0:
-                g_next = transpose_unit(i + 3)
-                codes_next = cpool.tile([128, 1024], U32, name="codes", tag="codes", align_bytes=64)
-                scales_next = cpool.tile([128, 1024], U8, name="scales", tag="scales", align_bytes=64)
-            extra = list(REGROUP.get(i, ()))
-            if kind == "edge":
-                agg = apool.tile([128, 2048], BF16, name="agg", tag="agg", align_bytes=64)
-            for aa in range(4):
-                acc = project(0 if kind == "node" else 1, codes, scales, aa)
-                acc_v = acc[:].rearrange("p (t c) -> p c t", t=4)
-                if kind == "node":
-                    j = j0 * 4 + aa
-                    nc.vector.tensor_tensor(out=nodeb[:, j * 512:(j + 1) * 512].rearrange("p (c t) -> p c t", t=4),
-                                            in0=acc_v, in1=bias32[:].unsqueeze(1).to_broadcast([128, 128, 4]), op=ADD)
-                else:
-                    nc.vector.tensor_tensor(out=agg[:, aa * 512:(aa + 1) * 512].rearrange("p (c t) -> p c t", t=4),
-                                            in0=acc_v,
-                                            in1=nodeb[:, j0 * 512:(j0 + 1) * 512].rearrange("p (c t) -> p c t", t=4),
-                                            op=ADD)
-                if aa % 2 == 0 and len(extra) > aa // 2:
-                    regroup(extra[aa // 2][0], extra[aa // 2][1])
-                if aa == 1 and i + 1 < njobs and i > 0:
-                    quantise_half(g_next, codes_next, scales_next, 0)
-                if aa == 3 and i + 1 < njobs and i > 0:
-                    quantise_half(g_next, codes_next, scales_next, 1)
-                if kind == "edge" and i == njobs - 1:
-                    if aa == 1:
-                        quantise_agg(agg, i, 0, 2)
-                    elif aa >= 2:
-                        quantise_agg(agg, i, aa, 1)
-                elif kind == "edge" and aa >= 2:
-                    quantise_agg(agg, i, (aa - 2) * 2, 2)
-                if aa == 3 and i in QF:
-                    h = QF[i]
-                    for r in range(2):
-                        c0 = h * 1024 + r * 512
+        groups = [[0]] + [[i] for i in range(1, GROUPS_OF_TWO_FROM)]
+        groups = groups + [[i, i + 1] for i in range(GROUPS_OF_TWO_FROM, len(jobs), 2)]
+        ready = {0: (codes, scales)}
+        for gi in range(len(groups)):
+            group = groups[gi]
+            following = groups[gi + 1] if gi + 1 < len(groups) else []
+            calls = []
+            if gi > 0:
+                for nxt in following:
+                    g_next = transpose_slab(nxt + 2)
+                    ready[nxt] = new_codes()
+                    calls.extend([(g_next, nxt, 0), (g_next, nxt, 1)])
+            total = STRIPS * len(group)
+            made = 0
+            strip = 0
+            for i in group:
+                job_kind, j0, j1 = jobs[i]
+                codes, scales = ready[i]
+                if job_kind == "edge":
+                    agg = apool.tile([P, STRIPS * BANK], BF16, name="agg", tag="agg", align_bytes=64)
+                for s in range(STRIPS):
+                    acc = project(0 if job_kind == "node" else 1, codes, scales, s)
+                    acc_v = acc[:].rearrange("p (t c) -> p c t", t=4)
+                    if job_kind == "node":
+                        j = j0 * STRIPS + s
+                        nc.vector.tensor_tensor(out=nodeb[:, j * BANK:(j + 1) * BANK].rearrange("p (c t) -> p c t", t=4),
+                                                in0=acc_v, in1=bias32[:].unsqueeze(1).to_broadcast([P, P, 4]), op=ADD)
+                    else:
+                        nc.vector.tensor_tensor(out=agg[:, s * BANK:(s + 1) * BANK].rearrange("p (c t) -> p c t", t=4),
+                                                in0=acc_v,
+                                                in1=nodeb[:, j0 * BANK:(j0 + 1) * BANK].rearrange("p (c t) -> p c t", t=4),
+                                                op=ADD)
+                    if s % 2 == 0 and 0 <= i - FWD_REGROUP_FROM < ATTRS // 2:
+                        regroup_fwd(2 * (i - FWD_REGROUP_FROM) + s // 2)
+                    while made < len(calls) and min(total - 1, (made + 1) * total // len(calls) - 2) <= strip:
+                        g_next, nxt, r = calls[made]
+                        quantise_pair_of_strips(g_next, ready[nxt][0], ready[nxt][1], r)
+                        made += 1
+                    if job_kind == "edge" and i == last_job:
+                        if s == 1:
+                            quantise_agg(agg, i, 0, 2)
+                        elif s >= 2:
+                            quantise_agg(agg, i, s, 1)
+                    elif job_kind == "edge" and s >= 2:
+                        quantise_agg(agg, i, (s - 2) * 2, 2)
+                    quarter = i - FWD_REGROUP_FROM - 1
+                    if s == STRIPS - 1 and 0 <= quarter < 4:
+                        c0 = quarter * 512
                         nc.vector.quantize_mx(out=f_codes[:, c0:c0 + 512].bitcast(FP8X4),
                                               scales=f_scales[:, c0:c0 + 512],
-                                              in_=f_grp[h][:, r * 2048:(r + 1) * 2048])
-                if i >= RSTART and aa in (LATE_SLOTS if i >= njobs - 2 else RSLOTS):
-                    rep_pair(i)
-            if i == 0:
-                g_next = transpose_unit(3)
-                codes_next = cpool.tile([128, 1024], U32, name="codes", tag="codes", align_bytes=64)
-                scales_next = cpool.tile([128, 1024], U8, name="scales", tag="scales", align_bytes=64)
-                for r in range(2):
-                    quantise_half(g_next, codes_next, scales_next, r)
-            if i + 1 < njobs:
-                codes, scales = codes_next, scales_next
-        for n in range(len(pending) - done[0]):
-            rep_pair(njobs)
+                                              in_=f_grp[quarter // 2][:, (quarter % 2) * 2048:(quarter % 2 + 1) * 2048])
+                    if i >= OUT_FROM and s in (OUT_BEHIND_STRIPS_AT_END if i >= last_job - 1 else OUT_BEHIND_STRIPS):
+                        second_product(i)
+                    strip += 1
+            if gi == 0:
+                for nxt in following:
+                    g_next = transpose_slab(nxt + 2)
+                    ready[nxt] = new_codes()
+                    for r in range(2):
+                        quantise_pair_of_strips(g_next, ready[nxt][0], ready[nxt][1], r)
+        for n in range(len(waiting) - taken[0]):
+            second_product(len(jobs))

@@ -13,22 +13,27 @@ ADD = mybir.AluOpType.add
 NODES, ATTRS, FEATS, PROJ, REP = 1024, 8, 1024, 512, 256
 FLOPS = 2 * (NODES * FEATS * PROJ + NODES * ATTRS * FEATS * PROJ + NODES * ATTRS * PROJ * REP)
 
-P = 128
+PARTS = 128
+PACK = 4
 STRIPS = 4
 SLAB = STRIPS * FEATS
 BANK = 512
 N_BANKS = 8
-BLOCKS = NODES // P
-HALF = SLAB // 2
+BLOCKS = NODES // PARTS
+PASSES = FEATS // (PARTS * PACK)
+DUO = 2 * FEATS
+DUO_WORDS = DUO // PACK
+FWD_DUO = 2 * PACK * REP
 
 SLABS_AHEAD = 6
 FWD_LOADED_BEHIND = (4, 5)
 FWD_REGROUP_FROM = 2
 FWD_QUANTISED_AFTER = {4: 0, 6: 1}
-OUT_FROM = 9
-GROUPS_OF_TWO_FROM = 6
+OUT_FROM = 7
 OUT_BEHIND_STRIPS = (0, 1, 2)
 OUT_BEHIND_STRIPS_AT_END = (1, 2, 3)
+WARM_SLABS = 3
+WARM_AT_START = 5
 
 
 def tile_attributegnn_pa_t_kernel(tc, image_features, edge_attributes, linear_w, linear_b, fwd_proj, out):
@@ -36,232 +41,233 @@ def tile_attributegnn_pa_t_kernel(tc, image_features, edge_attributes, linear_w,
     w_v = linear_w.rearrange("(q t) (h k) -> h q t k", t=STRIPS, h=2)
     img_v = image_features.rearrange("(c j) k -> c (j k)", j=BLOCKS)
     ea_v = edge_attributes.rearrange("(c j) a k -> c j (a k)", j=BLOCKS)
-    f_v = fwd_proj.rearrange("a (q t) r -> q a (t r)", t=4)
+    fwd_v = fwd_proj.rearrange("a (q t) r -> q a (t r)", t=PACK)
     out_v = out.rearrange("(c j) a r -> c j (a r)", j=BLOCKS)
-    b_v = linear_b.rearrange("(q t) -> q t", t=4)
+    bias_v = linear_b.rearrange("(q t) -> q t", t=PACK)
 
-    edge_jobs = [("edge", u // 2, u % 2) for u in range(2 * BLOCKS)]
+    edge_jobs = [("edge", n // 2, n % 2) for n in range(2 * BLOCKS)]
     jobs = [("node", 0, 0)] + edge_jobs[:BLOCKS] + [("node", 1, 0)] + edge_jobs[BLOCKS:]
     last_job = len(jobs) - 1
     slabs = [("w", 0), ("job", 0), ("w", 1)] + [("job", i) for i in range(1, len(jobs))]
 
     with ExitStack() as ctx:
         const = ctx.enter_context(tc.tile_pool(name="const", bufs=1))
-        xpool = ctx.enter_context(tc.tile_pool(name="xpool", bufs=SLABS_AHEAD))
-        gpool = ctx.enter_context(tc.tile_pool(name="gpool", bufs=4))
-        cpool = ctx.enter_context(tc.tile_pool(name="cpool", bufs=5))
-        apool = ctx.enter_context(tc.tile_pool(name="apool", bufs=3))
-        rpool = ctx.enter_context(tc.tile_pool(name="rpool", bufs=20))
-        opool = ctx.enter_context(tc.tile_pool(name="opool", bufs=3))
+        slab_pool = ctx.enter_context(tc.tile_pool(name="slab_pool", bufs=SLABS_AHEAD))
+        grouped_pool = ctx.enter_context(tc.tile_pool(name="grouped_pool", bufs=3))
+        code_pool = ctx.enter_context(tc.tile_pool(name="code_pool", bufs=3))
+        agg_pool = ctx.enter_context(tc.tile_pool(name="agg_pool", bufs=3))
+        agg_code_pool = ctx.enter_context(tc.tile_pool(name="agg_code_pool", bufs=16))
+        out_pool = ctx.enter_context(tc.tile_pool(name="out_pool", bufs=3))
         psum = ctx.enter_context(tc.psum_pool(name="psum", bufs=1))
         ctx.enter_context(tc.manual_schedule())
 
-        banks_used = [0]
+        banks_taken = [0]
 
         def next_bank():
-            k = banks_used[0] % N_BANKS
-            banks_used[0] += 1
-            return psum.tile([P, BANK], F32, name="bank%d" % k, tag="bank%d" % k)
+            n = banks_taken[0] % N_BANKS
+            banks_taken[0] += 1
+            return psum.tile([PARTS, BANK], F32, name="bank%d" % n, tag="bank%d" % n)
 
-        ident = const.tile([P, P], F32, name="ident")
+        ident = const.tile([PARTS, PARTS], F32, name="ident")
         make_identity(nc, ident[:])
-        bias_bf = const.tile([P, 4], BF16, name="bias_bf")
+        bias_bf = const.tile([PARTS, PACK], BF16, name="bias_bf")
         with nc.allow_non_contiguous_dma(reason="512 bias values, four to a partition"):
-            nc.scalar.dma_start(out=bias_bf[:], in_=b_v)
-        bias32 = const.tile([P, 4], F32, name="bias32")
-        nc.vector.tensor_copy(out=bias32[:], in_=bias_bf[:])
-        nodeb = const.tile([P, BLOCKS * BANK], F32, name="nodeb")
-        w_codes = [const.tile([P, SLAB // 4], U32, name="w_codes%d" % h, align_bytes=64) for h in range(2)]
-        w_scales = [const.tile([P, SLAB // 4], U8, name="w_scales%d" % h, align_bytes=64) for h in range(2)]
-        f_codes = const.tile([P, ATTRS * REP], U32, name="f_codes", align_bytes=64)
-        f_scales = const.tile([P, ATTRS * REP], U8, name="f_scales", align_bytes=64)
-        f_raw = [const.tile([P, 4 * 4 * REP], BF16, name="f_raw%d" % h) for h in range(2)]
-        f_grp = [const.tile([P, 4 * 4 * REP], BF16, name="f_grp%d" % h, align_bytes=64) for h in range(2)]
+            nc.scalar.dma_start(out=bias_bf[:], in_=bias_v)
+        bias = const.tile([PARTS, PACK], F32, name="bias")
+        nc.vector.tensor_copy(out=bias[:], in_=bias_bf[:])
+        node_term = const.tile([PARTS, BLOCKS * BANK], F32, name="node_term")
+        w_codes = [const.tile([PARTS, SLAB // PACK], U32, name="w_codes%d" % h, align_bytes=64) for h in range(2)]
+        w_scales = [const.tile([PARTS, SLAB // PACK], U8, name="w_scales%d" % h, align_bytes=64) for h in range(2)]
+        fwd_codes = const.tile([PARTS, ATTRS * REP], U32, name="fwd_codes", align_bytes=64)
+        fwd_scales = const.tile([PARTS, ATTRS * REP], U8, name="fwd_scales", align_bytes=64)
+        fwd_raw = [const.tile([PARTS, 2 * FWD_DUO], BF16, name="fwd_raw%d" % half) for half in range(2)]
+        fwd_grouped = [const.tile([PARTS, 2 * FWD_DUO], BF16, name="fwd_grouped%d" % half, align_bytes=64)
+                       for half in range(2)]
 
-        x_tiles = []
+        zeros = const.tile([PARTS, BANK], BF16, name="zeros")
+        nc.vector.memset(zeros[:], 0.0)
+
+        loaded = []
 
         def load_next_slab():
-            n = len(x_tiles)
+            n = len(loaded)
             if n >= len(slabs):
                 return
-            kind, idx = slabs[n]
-            x = xpool.tile([P, SLAB], BF16, name="x", tag="x")
+            kind, number = slabs[n]
+            slab = slab_pool.tile([PARTS, SLAB], BF16, name="slab", tag="slab")
             if kind == "w":
                 for t in range(STRIPS):
-                    nc.sync.dma_start(out=x[:, t * FEATS:(t + 1) * FEATS], in_=w_v[idx][:, t, :])
+                    nc.sync.dma_start(out=slab[:, t * FEATS:(t + 1) * FEATS], in_=w_v[number][:, t, :])
             else:
-                job_kind, j0, j1 = jobs[idx]
-                if job_kind == "node" and idx == 0:
-                    for t in range(STRIPS):
-                        c0 = j0 * SLAB + t * FEATS
-                        nc.sync.dma_start(out=x[:, t * FEATS:(t + 1) * FEATS], in_=img_v[:, c0:c0 + FEATS])
+                job_kind, first, half = jobs[number]
+                if job_kind == "node" and number == 0:
+                    for s in range(STRIPS):
+                        col = first * SLAB + s * FEATS
+                        nc.sync.dma_start(out=slab[:, s * FEATS:(s + 1) * FEATS], in_=img_v[:, col:col + FEATS])
                 elif job_kind == "node":
-                    nc.sync.dma_start(out=x[:], in_=img_v[:, j0 * SLAB:(j0 + 1) * SLAB])
+                    nc.sync.dma_start(out=slab[:], in_=img_v[:, first * SLAB:(first + 1) * SLAB])
                 else:
-                    nc.sync.dma_start(out=x[:], in_=ea_v[:, j0, j1 * SLAB:(j1 + 1) * SLAB])
-            x_tiles.append(x)
+                    nc.sync.dma_start(out=slab[:], in_=ea_v[:, first, half * SLAB:(half + 1) * SLAB])
+            loaded.append(slab)
             if n in FWD_LOADED_BEHIND:
-                h = FWD_LOADED_BEHIND.index(n)
-                nc.sync.dma_start(out=f_raw[h][:].rearrange("p (a s) -> p a s", a=4), in_=f_v[:, h * 4:(h + 1) * 4, :])
+                half = FWD_LOADED_BEHIND.index(n)
+                nc.sync.dma_start(out=fwd_raw[half][:].rearrange("q (s x) -> q s x", s=STRIPS),
+                                  in_=fwd_v[:, half * STRIPS:(half + 1) * STRIPS, :])
 
         def transpose_slab(n):
-            x32 = x_tiles[n][:].bitcast(F32)
-            g = gpool.tile([P, SLAB], BF16, name="g", tag="g", align_bytes=64)
-            g32 = g[:].bitcast(F32).rearrange("p (r g a c u) -> p r g a c u", r=2, g=2, a=2, c=P, u=2)
+            words = loaded[n][:].bitcast(F32)
+            grouped = grouped_pool.tile([PARTS, SLAB], BF16, name="grouped", tag="grouped", align_bytes=64)
+            grouped_words = grouped[:].bitcast(F32).rearrange("w (d g s c u) -> w d g s c u",
+                                                              d=2, g=PASSES, s=2, c=PARTS, u=2)
             for s in range(STRIPS):
-                xt = next_bank()
-                for piece in range(4):
-                    col = s * (FEATS // 2) + piece * P
-                    nc.tensor.transpose(xt[:, piece * P:(piece + 1) * P], x32[:, col:col + P], ident[:])
-                nc.scalar.copy(out=g32[:, s // 2, :, s % 2, :, :],
-                               in_=xt[:].rearrange("p (g u c) -> p g c u", g=2, u=2, c=P))
+                pieces = next_bank()
+                if n < WARM_SLABS:
+                    for warm in range(WARM_AT_START if n == 0 and s == 0 else 1):
+                        nc.tensor.matmul(out=pieces[:], lhsT=zeros[:, 0:PARTS], rhs=zeros[:], start=True, stop=True)
+                for piece in range(2 * PASSES):
+                    col = s * (FEATS // 2) + piece * PARTS
+                    nc.tensor.transpose(pieces[:, piece * PARTS:(piece + 1) * PARTS], words[:, col:col + PARTS],
+                                        ident[:])
+                nc.scalar.copy(out=grouped_words[:, s // 2, :, s % 2, :, :],
+                               in_=pieces[:].rearrange("w (g u c) -> w g c u", g=PASSES, u=2, c=PARTS))
             load_next_slab()
-            return g
+            return grouped
 
-        def quantise_pair_of_strips(g, codes, scales, r):
-            nc.vector.quantize_mx(out=codes[:, r * (HALF // 4):(r + 1) * (HALF // 4)].bitcast(FP8X4),
-                                  scales=scales[:, r * (HALF // 4):(r + 1) * (HALF // 4)],
-                                  in_=g[:, r * HALF:(r + 1) * HALF])
+        def quantise_duo(grouped, codes, scales, d):
+            nc.vector.quantize_mx(out=codes[:, d * DUO_WORDS:(d + 1) * DUO_WORDS].bitcast(FP8X4),
+                                  scales=scales[:, d * DUO_WORDS:(d + 1) * DUO_WORDS],
+                                  in_=grouped[:, d * DUO:(d + 1) * DUO])
 
         def new_codes():
-            codes = cpool.tile([P, SLAB // 4], U32, name="codes", tag="codes", align_bytes=64)
-            scales = cpool.tile([P, SLAB // 4], U8, name="scales", tag="scales", align_bytes=64)
+            codes = code_pool.tile([PARTS, SLAB // PACK], U32, name="codes", tag="codes", align_bytes=64)
+            scales = code_pool.tile([PARTS, SLAB // PACK], U8, name="scales", tag="scales", align_bytes=64)
             return codes, scales
 
-        def words_of(s, g):
-            return (s // 2) * 512 + g * 256 + (s % 2) * P
+        def first_word(s, g):
+            return (s // 2) * DUO_WORDS + g * 2 * PARTS + (s % 2) * PARTS
 
-        def project(h, codes, scales, s):
+        def first_product(h, codes, scales, s):
             acc = next_bank()
             for t in range(STRIPS):
-                for g in range(2):
-                    wc = words_of(t, g)
-                    dc = words_of(s, g)
-                    nc.tensor.matmul_mx(out=acc[:, t * P:(t + 1) * P],
-                                        lhsT=w_codes[h][:, wc:wc + P].bitcast(FP8X4),
-                                        lhsT_scale=w_scales[h][:, wc:wc + P],
-                                        rhs=codes[:, dc:dc + P].bitcast(FP8X4),
-                                        rhs_scale=scales[:, dc:dc + P],
-                                        start=(g == 0), stop=(g == 1))
+                for g in range(PASSES):
+                    w_col = first_word(t, g)
+                    col = first_word(s, g)
+                    nc.tensor.matmul_mx(out=acc[:, t * PARTS:(t + 1) * PARTS],
+                                        lhsT=w_codes[h][:, w_col:w_col + PARTS].bitcast(FP8X4),
+                                        lhsT_scale=w_scales[h][:, w_col:w_col + PARTS],
+                                        rhs=codes[:, col:col + PARTS].bitcast(FP8X4),
+                                        rhs_scale=scales[:, col:col + PARTS],
+                                        start=(g == 0), stop=(g == PASSES - 1))
             return acc
 
         waiting = []
         taken = [0]
-        o_tiles = {}
+        out_tiles = {}
 
         def quantise_agg(agg, i, s0, n_strips):
-            job_kind, j0, j1 = jobs[i]
-            a_codes = rpool.tile([P, 2 * P], U32, name="a_codes", tag="a_codes", align_bytes=64)
-            a_scales = rpool.tile([P, 2 * P], U8, name="a_scales", tag="a_scales", align_bytes=64)
-            nc.vector.quantize_mx(out=a_codes[:, 0:n_strips * P].bitcast(FP8X4), scales=a_scales[:, 0:n_strips * P],
+            job_kind, j, half = jobs[i]
+            agg_codes = agg_code_pool.tile([PARTS, 2 * PARTS], U32, name="agg_codes", tag="agg_codes", align_bytes=64)
+            agg_scales = agg_code_pool.tile([PARTS, 2 * PARTS], U8, name="agg_scales", tag="agg_scales",
+                                            align_bytes=64)
+            nc.vector.quantize_mx(out=agg_codes[:, 0:n_strips * PARTS].bitcast(FP8X4),
+                                  scales=agg_scales[:, 0:n_strips * PARTS],
                                   in_=agg[:, s0 * BANK:(s0 + n_strips) * BANK])
-            waiting.append((a_codes, a_scales, i, j0, j1, s0, n_strips))
+            waiting.append((agg_codes, agg_scales, i, j, half, s0, n_strips))
 
         def second_product(now):
             if taken[0] >= len(waiting):
                 return
-            a_codes, a_scales, i, j, half, s0, n_strips = waiting[taken[0]]
+            agg_codes, agg_scales, i, j, half, s0, n_strips = waiting[taken[0]]
             if i >= now:
                 return
             taken[0] += 1
             if s0 == 0:
-                o_tiles[i] = opool.tile([P, STRIPS * REP], F32, name="o_sb", tag="o_sb")
-            o_sb = o_tiles[i]
-            o = next_bank()
+                out_tiles[i] = out_pool.tile([PARTS, STRIPS * REP], F32, name="out_rows", tag="out_rows")
+            out_rows = out_tiles[i]
+            sums = next_bank()
             for s in range(n_strips):
                 a = half * STRIPS + s0 + s
-                nc.tensor.matmul_mx(out=o[:, s * REP:(s + 1) * REP],
-                                    lhsT=a_codes[:, s * P:(s + 1) * P].bitcast(FP8X4),
-                                    lhsT_scale=a_scales[:, s * P:(s + 1) * P],
-                                    rhs=f_codes[:, a * REP:(a + 1) * REP].bitcast(FP8X4),
-                                    rhs_scale=f_scales[:, a * REP:(a + 1) * REP],
+                nc.tensor.matmul_mx(out=sums[:, s * REP:(s + 1) * REP],
+                                    lhsT=agg_codes[:, s * PARTS:(s + 1) * PARTS].bitcast(FP8X4),
+                                    lhsT_scale=agg_scales[:, s * PARTS:(s + 1) * PARTS],
+                                    rhs=fwd_codes[:, a * REP:(a + 1) * REP].bitcast(FP8X4),
+                                    rhs_scale=fwd_scales[:, a * REP:(a + 1) * REP],
                                     start=True, stop=True)
-            nc.scalar.copy(out=o_sb[:, s0 * REP:(s0 + n_strips) * REP], in_=o[:, 0:n_strips * REP])
+            nc.scalar.copy(out=out_rows[:, s0 * REP:(s0 + n_strips) * REP], in_=sums[:, 0:n_strips * REP])
             if i == last_job:
-                c0 = (half * STRIPS + s0) * REP
-                nc.scalar.dma_start(out=out_v[:, j, c0:c0 + n_strips * REP],
-                                    in_=o_sb[:, s0 * REP:(s0 + n_strips) * REP])
+                col = (half * STRIPS + s0) * REP
+                nc.scalar.dma_start(out=out_v[:, j, col:col + n_strips * REP],
+                                    in_=out_rows[:, s0 * REP:(s0 + n_strips) * REP])
             elif s0 + n_strips == STRIPS:
-                nc.scalar.dma_start(out=out_v[:, j, half * STRIPS * REP:(half + 1) * STRIPS * REP], in_=o_sb[:])
+                nc.scalar.dma_start(out=out_v[:, j, half * STRIPS * REP:(half + 1) * STRIPS * REP], in_=out_rows[:])
 
         def regroup_fwd(a):
-            cols = slice((a % 4) * 4 * REP, (a % 4 + 1) * 4 * REP)
-            nc.scalar.copy(out=f_grp[a // 4][:, cols].rearrange("p (c i t) -> p c t i", t=4, i=4),
-                           in_=f_raw[a // 4][:, cols].rearrange("p (t c i) -> p c t i", t=4, i=4))
+            cols = slice((a % STRIPS) * PACK * REP, (a % STRIPS + 1) * PACK * REP)
+            nc.scalar.copy(out=fwd_grouped[a // STRIPS][:, cols].rearrange("q (m v t) -> q m t v", t=PACK, v=4),
+                           in_=fwd_raw[a // STRIPS][:, cols].rearrange("q (t m v) -> q m t v", t=PACK, v=4))
 
         for n in range(SLABS_AHEAD):
             load_next_slab()
 
-        g = transpose_slab(0)
-        for r in range(2):
-            quantise_pair_of_strips(g, w_codes[0], w_scales[0], r)
-        g = transpose_slab(1)
+        grouped = transpose_slab(0)
+        for d in range(2):
+            quantise_duo(grouped, w_codes[0], w_scales[0], d)
+        grouped = transpose_slab(1)
         codes, scales = new_codes()
-        for r in range(2):
-            quantise_pair_of_strips(g, codes, scales, r)
-        g = transpose_slab(2)
-        for r in range(2):
-            quantise_pair_of_strips(g, w_codes[1], w_scales[1], r)
+        for d in range(2):
+            quantise_duo(grouped, codes, scales, d)
+        grouped = transpose_slab(2)
+        for d in range(2):
+            quantise_duo(grouped, w_codes[1], w_scales[1], d)
 
-        groups = [[0]] + [[i] for i in range(1, GROUPS_OF_TWO_FROM)]
-        groups = groups + [[i, i + 1] for i in range(GROUPS_OF_TWO_FROM, len(jobs), 2)]
-        ready = {0: (codes, scales)}
-        for gi in range(len(groups)):
-            group = groups[gi]
-            following = groups[gi + 1] if gi + 1 < len(groups) else []
-            calls = []
-            if gi > 0:
-                for nxt in following:
-                    g_next = transpose_slab(nxt + 2)
-                    ready[nxt] = new_codes()
-                    calls.extend([(g_next, nxt, 0), (g_next, nxt, 1)])
-            total = STRIPS * len(group)
-            made = 0
-            strip = 0
-            for i in group:
-                job_kind, j0, j1 = jobs[i]
-                codes, scales = ready[i]
-                if job_kind == "edge":
-                    agg = apool.tile([P, STRIPS * BANK], BF16, name="agg", tag="agg", align_bytes=64)
-                for s in range(STRIPS):
-                    acc = project(0 if job_kind == "node" else 1, codes, scales, s)
-                    acc_v = acc[:].rearrange("p (t c) -> p c t", t=4)
-                    if job_kind == "node":
-                        j = j0 * STRIPS + s
-                        nc.vector.tensor_tensor(out=nodeb[:, j * BANK:(j + 1) * BANK].rearrange("p (c t) -> p c t", t=4),
-                                                in0=acc_v, in1=bias32[:].unsqueeze(1).to_broadcast([P, P, 4]), op=ADD)
-                    else:
-                        nc.vector.tensor_tensor(out=agg[:, s * BANK:(s + 1) * BANK].rearrange("p (c t) -> p c t", t=4),
-                                                in0=acc_v,
-                                                in1=nodeb[:, j0 * BANK:(j0 + 1) * BANK].rearrange("p (c t) -> p c t", t=4),
-                                                op=ADD)
-                    if s % 2 == 0 and 0 <= i - FWD_REGROUP_FROM < ATTRS // 2:
-                        regroup_fwd(2 * (i - FWD_REGROUP_FROM) + s // 2)
-                    while made < len(calls) and min(total - 1, (made + 1) * total // len(calls) - 2) <= strip:
-                        g_next, nxt, r = calls[made]
-                        quantise_pair_of_strips(g_next, ready[nxt][0], ready[nxt][1], r)
-                        made += 1
-                    if job_kind == "edge" and i == last_job:
-                        if s == 1:
-                            quantise_agg(agg, i, 0, 2)
-                        elif s >= 2:
-                            quantise_agg(agg, i, s, 1)
-                    elif job_kind == "edge" and s >= 2:
-                        quantise_agg(agg, i, (s - 2) * 2, 2)
-                    quarter = i - FWD_REGROUP_FROM - 1
-                    if s == STRIPS - 1 and 0 <= quarter < 4:
-                        c0 = quarter * 512
-                        nc.vector.quantize_mx(out=f_codes[:, c0:c0 + 512].bitcast(FP8X4),
-                                              scales=f_scales[:, c0:c0 + 512],
-                                              in_=f_grp[quarter // 2][:, (quarter % 2) * 2048:(quarter % 2 + 1) * 2048])
-                    if i >= OUT_FROM and s in (OUT_BEHIND_STRIPS_AT_END if i >= last_job - 1 else OUT_BEHIND_STRIPS):
-                        second_product(i)
-                    strip += 1
-            if gi == 0:
-                for nxt in following:
-                    g_next = transpose_slab(nxt + 2)
-                    ready[nxt] = new_codes()
-                    for r in range(2):
-                        quantise_pair_of_strips(g_next, ready[nxt][0], ready[nxt][1], r)
+        for i in range(len(jobs)):
+            job_kind, first, half = jobs[i]
+            next_first = 0 < i < last_job
+            if next_first:
+                grouped_next = transpose_slab(i + 3)
+                codes_next, scales_next = new_codes()
+            if job_kind == "edge":
+                agg = agg_pool.tile([PARTS, STRIPS * BANK], BF16, name="agg", tag="agg", align_bytes=64)
+            for s in range(STRIPS):
+                acc = first_product(0 if job_kind == "node" else 1, codes, scales, s)
+                acc_ct = acc[:].rearrange("q (t c) -> q c t", t=PACK)
+                if job_kind == "node":
+                    j = first * STRIPS + s
+                    nc.vector.tensor_tensor(
+                        out=node_term[:, j * BANK:(j + 1) * BANK].rearrange("q (c t) -> q c t", t=PACK),
+                        in0=acc_ct, in1=bias[:].unsqueeze(1).to_broadcast([PARTS, PARTS, PACK]), op=ADD)
+                else:
+                    nc.vector.tensor_tensor(
+                        out=agg[:, s * BANK:(s + 1) * BANK].rearrange("q (c t) -> q c t", t=PACK),
+                        in0=acc_ct,
+                        in1=node_term[:, first * BANK:(first + 1) * BANK].rearrange("q (c t) -> q c t", t=PACK),
+                        op=ADD)
+                if s % 2 == 0 and 0 <= i - FWD_REGROUP_FROM < ATTRS // 2:
+                    regroup_fwd(2 * (i - FWD_REGROUP_FROM) + s // 2)
+                if next_first and s % 2 == 1:
+                    quantise_duo(grouped_next, codes_next, scales_next, s // 2)
+                if job_kind == "edge" and i == last_job:
+                    if s == 1:
+                        quantise_agg(agg, i, 0, 2)
+                    elif s >= 2:
+                        quantise_agg(agg, i, s, 1)
+                elif job_kind == "edge" and s >= 2:
+                    quantise_agg(agg, i, (s - 2) * 2, 2)
+                if s == STRIPS - 1 and i in FWD_QUANTISED_AFTER:
+                    fwd_half = FWD_QUANTISED_AFTER[i]
+                    for d in range(2):
+                        col = (2 * fwd_half + d) * (FWD_DUO // PACK)
+                        nc.vector.quantize_mx(out=fwd_codes[:, col:col + FWD_DUO // PACK].bitcast(FP8X4),
+                                              scales=fwd_scales[:, col:col + FWD_DUO // PACK],
+                                              in_=fwd_grouped[fwd_half][:, d * FWD_DUO:(d + 1) * FWD_DUO])
+                if i >= OUT_FROM and s in (OUT_BEHIND_STRIPS_AT_END if i >= last_job - 1 else OUT_BEHIND_STRIPS):
+                    second_product(i)
+            if i == 0:
+                grouped_next = transpose_slab(3)
+                codes_next, scales_next = new_codes()
+                for d in range(2):
+                    quantise_duo(grouped_next, codes_next, scales_next, d)
+            if i < last_job:
+                codes, scales = codes_next, scales_next
         for n in range(len(waiting) - taken[0]):
             second_product(len(jobs))

@@ -68,6 +68,8 @@ def tile_attributegnn_pa_t_kernel(tc, image_features, edge_attributes, linear_w,
             banks_taken[0] += 1
             return psum.tile([PARTS, BANK], F32, name="bank%d" % n, tag="bank%d" % n)
 
+        zeros = const.tile([PARTS, BANK], BF16, name="zeros")
+        nc.vector.memset(zeros[:], 0.0)
         ident = const.tile([PARTS, PARTS], F32, name="ident")
         make_identity(nc, ident[:])
         bias_bf = const.tile([PARTS, PACK], BF16, name="bias_bf")
@@ -83,9 +85,6 @@ def tile_attributegnn_pa_t_kernel(tc, image_features, edge_attributes, linear_w,
         fwd_raw = [const.tile([PARTS, 2 * FWD_DUO], BF16, name="fwd_raw%d" % half) for half in range(2)]
         fwd_grouped = [const.tile([PARTS, 2 * FWD_DUO], BF16, name="fwd_grouped%d" % half, align_bytes=64)
                        for half in range(2)]
-
-        zeros = const.tile([PARTS, BANK], BF16, name="zeros")
-        nc.vector.memset(zeros[:], 0.0)
 
         loaded = []
 

from contextlib import ExitStack

import concourse.mybir as mybir
from concourse.masks import make_identity

F32 = mybir.dt.float32
BF16 = mybir.dt.bfloat16
U32 = mybir.dt.uint32
U8 = mybir.dt.uint8
FP8X4 = mybir.dt.float8_e4m3fn_x4
ADD = mybir.AluOpType.add

NODES, ATTRS, FEATS, PROJ, REP = 1024, 8, 1024, 512, 256
FLOPS = 2 * (NODES * FEATS * PROJ + NODES * ATTRS * FEATS * PROJ + NODES * ATTRS * PROJ * REP)

PARTS = 128
PACK = 4
STRIPS = 4
SLAB = STRIPS * FEATS
BANK = 512
N_BANKS = 8
BLOCKS = NODES // PARTS
PASSES = FEATS // (PARTS * PACK)
DUO = 2 * FEATS
DUO_WORDS = DUO // PACK
FWD_DUO = 2 * PACK * REP

SLABS_AHEAD = 6
FWD_LOADED_BEHIND = (4, 5)
FWD_REGROUP_FROM = 2
FWD_QUANTISED_AFTER = {4: 0, 6: 1}
OUT_FROM = 7
OUT_BEHIND_STRIPS = (0, 1, 2)
OUT_BEHIND_STRIPS_AT_END = (1, 2, 3)
WARM_SLABS = 3
WARM_AT_START = 5


def tile_attributegnn_pa_t_kernel(tc, image_features, edge_attributes, linear_w, linear_b, fwd_proj, out):
    nc = tc.nc
    w_v = linear_w.rearrange("(q t) (h k) -> h q t k", t=STRIPS, h=2)
    img_v = image_features.rearrange("(c j) k -> c (j k)", j=BLOCKS)
    ea_v = edge_attributes.rearrange("(c j) a k -> c j (a k)", j=BLOCKS)
    fwd_v = fwd_proj.rearrange("a (q t) r -> q a (t r)", t=PACK)
    out_v = out.rearrange("(c j) a r -> c j (a r)", j=BLOCKS)
    bias_v = linear_b.rearrange("(q t) -> q t", t=PACK)

    edge_jobs = [("edge", n // 2, n % 2) for n in range(2 * BLOCKS)]
    jobs = [("node", 0, 0)] + edge_jobs[:BLOCKS] + [("node", 1, 0)] + edge_jobs[BLOCKS:]
    last_job = len(jobs) - 1
    slabs = [("w", 0), ("job", 0), ("w", 1)] + [("job", i) for i in range(1, len(jobs))]

    with ExitStack() as ctx:
        const = ctx.enter_context(tc.tile_pool(name="const", bufs=1))
        slab_pool = ctx.enter_context(tc.tile_pool(name="slab_pool", bufs=SLABS_AHEAD))
        grouped_pool = ctx.enter_context(tc.tile_pool(name="grouped_pool", bufs=3))
        code_pool = ctx.enter_context(tc.tile_pool(name="code_pool", bufs=3))
        agg_pool = ctx.enter_context(tc.tile_pool(name="agg_pool", bufs=3))
        agg_code_pool = ctx.enter_context(tc.tile_pool(name="agg_code_pool", bufs=16))
        out_pool = ctx.enter_context(tc.tile_pool(name="out_pool", bufs=3))
        psum = ctx.enter_context(tc.psum_pool(name="psum", bufs=1))
        ctx.enter_context(tc.manual_schedule())

        banks_taken = [0]

        def next_bank():
            n = banks_taken[0] % N_BANKS
            banks_taken[0] += 1
            return psum.tile([PARTS, BANK], F32, name="bank%d" % n, tag="bank%d" % n)

        zeros = const.tile([PARTS, BANK], BF16, name="zeros")
        nc.vector.memset(zeros[:], 0.0)
        ident = const.tile([PARTS, PARTS], F32, name="ident")
        make_identity(nc, ident[:])
        bias_bf = const.tile([PARTS, PACK], BF16, name="bias_bf")
        with nc.allow_non_contiguous_dma(reason="512 bias values, four to a partition"):
            nc.scalar.dma_start(out=bias_bf[:], in_=bias_v)
        bias = const.tile([PARTS, PACK], F32, name="bias")
        nc.vector.tensor_copy(out=bias[:], in_=bias_bf[:])
        node_term = const.tile([PARTS, BLOCKS * BANK], F32, name="node_term")
        w_codes = [const.tile([PARTS, SLAB // PACK], U32, name="w_codes%d" % h, align_bytes=64) for h in range(2)]
        w_scales = [const.tile([PARTS, SLAB // PACK], U8, name="w_scales%d" % h, align_bytes=64) for h in range(2)]
        fwd_codes = const.tile([PARTS, ATTRS * REP], U32, name="fwd_codes", align_bytes=64)
        fwd_scales = const.tile([PARTS, ATTRS * REP], U8, name="fwd_scales", align_bytes=64)
        fwd_raw = [const.tile([PARTS, 2 * FWD_DUO], BF16, name="fwd_raw%d" % half) for half in range(2)]
        fwd_grouped = [const.tile([PARTS, 2 * FWD_DUO], BF16, name="fwd_grouped%d" % half, align_bytes=64)
                       for half in range(2)]

        loaded = []

        def load_next_slab():
            n = len(loaded)
            if n >= len(slabs):
                return
            kind, number = slabs[n]
            slab = slab_pool.tile([PARTS, SLAB], BF16, name="slab", tag="slab")
            if kind == "w":
                for t in range(STRIPS):
                    nc.sync.dma_start(out=slab[:, t * FEATS:(t + 1) * FEATS], in_=w_v[number][:, t, :])
            else:
                job_kind, first, half = jobs[number]
                if job_kind == "node" and number == 0:
                    for s in range(STRIPS):
                        col = first * SLAB + s * FEATS
                        nc.sync.dma_start(out=slab[:, s * FEATS:(s + 1) * FEATS], in_=img_v[:, col:col + FEATS])
                elif job_kind == "node":
                    nc.sync.dma_start(out=slab[:], in_=img_v[:, first * SLAB:(first + 1) * SLAB])
                else:
                    nc.sync.dma_start(out=slab[:], in_=ea_v[:, first, half * SLAB:(half + 1) * SLAB])
            loaded.append(slab)
            if n in FWD_LOADED_BEHIND:
                half = FWD_LOADED_BEHIND.index(n)
                nc.sync.dma_start(out=fwd_raw[half][:].rearrange("q (s x) -> q s x", s=STRIPS),
                                  in_=fwd_v[:, half * STRIPS:(half + 1) * STRIPS, :])

        def transpose_slab(n):
            words = loaded[n][:].bitcast(F32)
            grouped = grouped_pool.tile([PARTS, SLAB], BF16, name="grouped", tag="grouped", align_bytes=64)
            grouped_words = grouped[:].bitcast(F32).rearrange("w (d g s c u) -> w d g s c u",
                                                              d=2, g=PASSES, s=2, c=PARTS, u=2)
            for s in range(STRIPS):
                pieces = next_bank()
                if n < WARM_SLABS:
                    for warm in range(WARM_AT_START if n == 0 and s == 0 else 1):
                        nc.tensor.matmul(out=pieces[:], lhsT=zeros[:, 0:PARTS], rhs=zeros[:], start=True, stop=True)
                for piece in range(2 * PASSES):
                    col = s * (FEATS // 2) + piece * PARTS
                    nc.tensor.transpose(pieces[:, piece * PARTS:(piece + 1) * PARTS], words[:, col:col + PARTS],
                                        ident[:])
                nc.scalar.copy(out=grouped_words[:, s // 2, :, s % 2, :, :],
                               in_=pieces[:].rearrange("w (g u c) -> w g c u", g=PASSES, u=2, c=PARTS))
            load_next_slab()
            return grouped

        def quantise_duo(grouped, codes, scales, d):
            nc.vector.quantize_mx(out=codes[:, d * DUO_WORDS:(d + 1) * DUO_WORDS].bitcast(FP8X4),
                                  scales=scales[:, d * DUO_WORDS:(d + 1) * DUO_WORDS],
                                  in_=grouped[:, d * DUO:(d + 1) * DUO])

        def new_codes():
            codes = code_pool.tile([PARTS, SLAB // PACK], U32, name="codes", tag="codes", align_bytes=64)
            scales = code_pool.tile([PARTS, SLAB // PACK], U8, name="scales", tag="scales", align_bytes=64)
            return codes, scales

        def first_word(s, g):
            return (s // 2) * DUO_WORDS + g * 2 * PARTS + (s % 2) * PARTS

        def first_product(h, codes, scales, s):
            acc = next_bank()
            for t in range(STRIPS):
                for g in range(PASSES):
                    w_col = first_word(t, g)
                    col = first_word(s, g)
                    nc.tensor.matmul_mx(out=acc[:, t * PARTS:(t + 1) * PARTS],
                                        lhsT=w_codes[h][:, w_col:w_col + PARTS].bitcast(FP8X4),
                                        lhsT_scale=w_scales[h][:, w_col:w_col + PARTS],
                                        rhs=codes[:, col:col + PARTS].bitcast(FP8X4),
                                        rhs_scale=scales[:, col:col + PARTS],
                                        start=(g == 0), stop=(g == PASSES - 1))
            return acc

        waiting = []
        taken = [0]
        out_tiles = {}

        def quantise_agg(agg, i, s0, n_strips):
            job_kind, j, half = jobs[i]
            agg_codes = agg_code_pool.tile([PARTS, 2 * PARTS], U32, name="agg_codes", tag="agg_codes", align_bytes=64)
            agg_scales = agg_code_pool.tile([PARTS, 2 * PARTS], U8, name="agg_scales", tag="agg_scales",
                                            align_bytes=64)
            nc.vector.quantize_mx(out=agg_codes[:, 0:n_strips * PARTS].bitcast(FP8X4),
                                  scales=agg_scales[:, 0:n_strips * PARTS],
                                  in_=agg[:, s0 * BANK:(s0 + n_strips) * BANK])
            waiting.append((agg_codes, agg_scales, i, j, half, s0, n_strips))

        def second_product(now):
            if taken[0] >= len(waiting):
                return
            agg_codes, agg_scales, i, j, half, s0, n_strips = waiting[taken[0]]
            if i >= now:
                return
            taken[0] += 1
            if s0 == 0:
                out_tiles[i] = out_pool.tile([PARTS, STRIPS * REP], F32, name="out_rows", tag="out_rows")
            out_rows = out_tiles[i]
            sums = next_bank()
            for s in range(n_strips):
                a = half * STRIPS + s0 + s
                nc.tensor.matmul_mx(out=sums[:, s * REP:(s + 1) * REP],
                                    lhsT=agg_codes[:, s * PARTS:(s + 1) * PARTS].bitcast(FP8X4),
                                    lhsT_scale=agg_scales[:, s * PARTS:(s + 1) * PARTS],
                                    rhs=fwd_codes[:, a * REP:(a + 1) * REP].bitcast(FP8X4),
                                    rhs_scale=fwd_scales[:, a * REP:(a + 1) * REP],
                                    start=True, stop=True)
            nc.scalar.copy(out=out_rows[:, s0 * REP:(s0 + n_strips) * REP], in_=sums[:, 0:n_strips * REP])
            if i == last_job:
                col = (half * STRIPS + s0) * REP
                nc.scalar.dma_start(out=out_v[:, j, col:col + n_strips * REP],
                                    in_=out_rows[:, s0 * REP:(s0 + n_strips) * REP])
            elif s0 + n_strips == STRIPS:
                nc.scalar.dma_start(out=out_v[:, j, half * STRIPS * REP:(half + 1) * STRIPS * REP], in_=out_rows[:])

        def regroup_fwd(a):
            cols = slice((a % STRIPS) * PACK * REP, (a % STRIPS + 1) * PACK * REP)
            nc.scalar.copy(out=fwd_grouped[a // STRIPS][:, cols].rearrange("q (m v t) -> q m t v", t=PACK, v=4),
                           in_=fwd_raw[a // STRIPS][:, cols].rearrange("q (t m v) -> q m t v", t=PACK, v=4))

        for n in range(SLABS_AHEAD):
            load_next_slab()

        grouped = transpose_slab(0)
        for d in range(2):
            quantise_duo(grouped, w_codes[0], w_scales[0], d)
        grouped = transpose_slab(1)
        codes, scales = new_codes()
        for d in range(2):
            quantise_duo(grouped, codes, scales, d)
        grouped = transpose_slab(2)
        for d in range(2):
            quantise_duo(grouped, w_codes[1], w_scales[1], d)

        for i in range(len(jobs)):
            job_kind, first, half = jobs[i]
            next_first = 0 < i < last_job
            if next_first:
                grouped_next = transpose_slab(i + 3)
                codes_next, scales_next = new_codes()
            if job_kind == "edge":
                agg = agg_pool.tile([PARTS, STRIPS * BANK], BF16, name="agg", tag="agg", align_bytes=64)
            for s in range(STRIPS):
                acc = first_product(0 if job_kind == "node" else 1, codes, scales, s)
                acc_ct = acc[:].rearrange("q (t c) -> q c t", t=PACK)
                if job_kind == "node":
                    j = first * STRIPS + s
                    nc.vector.tensor_tensor(
                        out=node_term[:, j * BANK:(j + 1) * BANK].rearrange("q (c t) -> q c t", t=PACK),
                        in0=acc_ct, in1=bias[:].unsqueeze(1).to_broadcast([PARTS, PARTS, PACK]), op=ADD)
                else:
                    nc.vector.tensor_tensor(
                        out=agg[:, s * BANK:(s + 1) * BANK].rearrange("q (c t) -> q c t", t=PACK),
                        in0=acc_ct,
                        in1=node_term[:, first * BANK:(first + 1) * BANK].rearrange("q (c t) -> q c t", t=PACK),
                        op=ADD)
                if s % 2 == 0 and 0 <= i - FWD_REGROUP_FROM < ATTRS // 2:
                    regroup_fwd(2 * (i - FWD_REGROUP_FROM) + s // 2)
                if next_first and s % 2 == 1:
                    quantise_duo(grouped_next, codes_next, scales_next, s // 2)
                if job_kind == "edge" and i == last_job:
                    if s == 1:
                        quantise_agg(agg, i, 0, 2)
                    elif s >= 2:
                        quantise_agg(agg, i, s, 1)
                elif job_kind == "edge" and s >= 2:
                    quantise_agg(agg, i, (s - 2) * 2, 2)
                if s == STRIPS - 1 and i in FWD_QUANTISED_AFTER:
                    fwd_half = FWD_QUANTISED_AFTER[i]
                    for d in range(2):
                        col = (2 * fwd_half + d) * (FWD_DUO // PACK)
                        nc.vector.quantize_mx(out=fwd_codes[:, col:col + FWD_DUO // PACK].bitcast(FP8X4),
                                              scales=fwd_scales[:, col:col + FWD_DUO // PACK],
                                              in_=fwd_grouped[fwd_half][:, d * FWD_DUO:(d + 1) * FWD_DUO])
                if i >= OUT_FROM and s in (OUT_BEHIND_STRIPS_AT_END if i >= last_job - 1 else OUT_BEHIND_STRIPS):
                    second_product(i)
            if i == 0:
                grouped_next = transpose_slab(3)
                codes_next, scales_next = new_codes()
                for d in range(2):
                    quantise_duo(grouped_next, codes_next, scales_next, d)
            if i < last_job:
                codes, scales = codes_next, scales_next
        for n in range(len(waiting) - taken[0]):
            second_product(len(jobs))
